import numpy as np
import ml_dtypes


def mxq(x, axis, fmt="e4m3"):
    dtype, down = {"e4m3": (ml_dtypes.float8_e4m3fn, 7), "e5m2": (ml_dtypes.float8_e5m2, 14)}[fmt]
    v = np.moveaxis(np.asarray(x, np.float32).astype(ml_dtypes.bfloat16).astype(np.float64), axis, -1)
    blocks = v.reshape(v.shape[:-1] + (-1, 32))
    amax = np.abs(blocks).max(-1, keepdims=True)
    byte = np.maximum(np.where(amax > 0, np.frexp(amax)[1] - 1 + 127, 0) - down, 1)
    scale = np.exp2(byte - 127.0)
    codes = (blocks / scale).astype(np.float32).astype(dtype).astype(np.float64)
    return np.moveaxis((codes * scale).reshape(v.shape), -1, axis)


WIDE = False


def mx_kscale(k):
    if not WIDE:
        return np.ones(k)
    levels = np.array([10, -10, 5, -5, 0])
    a = np.random.permutation(np.resize(levels, k // 512 * 4)).reshape(k // 512, 4)
    idx = np.arange(k)
    return np.exp2(a[idx // 512, idx % 128 // 32])


BF16 = ml_dtypes.bfloat16


def bf(x):
    return np.asarray(x, np.float32).astype(BF16)


def f64(x):
    return np.asarray(x).astype(np.float64)


T, K, E, H, KVH, D = 512, 1024, 2048, 16, 4, 128
EPS = 1e-05


def rmsnorm(x, w):
    var = np.mean(np.square(x), axis=-1, keepdims=True)
    return x * (1.0 / np.sqrt(var + EPS)) * w


def setup_inputs():
    s = mx_kscale(E)
    return {"hidden_states": bf(np.random.standard_normal((T, E)) * s),
            "Wq": bf(np.random.standard_normal((H * D, E)) / np.sqrt(E) / s),
            "q_norm_w": bf(1.5 + 0.1 * np.random.standard_normal(D))}


def reference(hidden_states, Wq, q_norm_w):
    q = mxq(f64(hidden_states), 1, "e4m3") @ mxq(f64(Wq), 1, "e4m3").T
    qh = rmsnorm(q.reshape(T, H, D), f64(q_norm_w))
    return qh.transpose(1, 0, 2)

@@ -1,0 +1,168 @@
+import concourse.mybir as mybir
+from concourse.masks import make_identity
+
+F32 = mybir.dt.float32
+BF16 = mybir.dt.bfloat16
+U32 = mybir.dt.uint32
+U8 = mybir.dt.uint8
+FP8X4 = mybir.dt.float8_e4m3fn_x4
+ACT = mybir.ActivationFunctionType
+ALU = mybir.AluOpType
+
+P = 128
+TOKENS, EMBED, HEADS, HEAD_DIM = 512, 2048, 16, 128
+EPS = 1e-05
+
+K_PASS = 4 * P
+PASSES = EMBED // K_PASS
+ROW_WORDS = EMBED // 2
+PASS_WORDS = K_PASS // 2
+
+UNIT_ROWS = 2 * P
+TOKEN_UNITS = TOKENS // UNIT_ROWS
+TOKEN_TILES = TOKENS // P
+WEIGHT_UNITS = HEADS * HEAD_DIM // UNIT_ROWS
+UNIT_HEADS = UNIT_ROWS // HEAD_DIM
+
+LEAD = 2
+
+FLOPS = 2 * TOKENS * EMBED * HEADS * HEAD_DIM
+
+
+def tile_combcrossattention_pa_kernel(tc, hidden_states, Wq, q_norm_w, out):
+    nc = tc.nc
+
+    with (
+        tc.tile_pool(name="consts", bufs=1) as consts,
+        tc.tile_pool(name="raw", bufs=1) as raw_pool,
+        tc.tile_pool(name="quantised", bufs=1) as quantised,
+        tc.tile_pool(name="grouped", bufs=2 * PASSES) as grouped_pool,
+        tc.tile_pool(name="stats", bufs=4) as stats,
+        tc.tile_pool(name="results", bufs=3) as results,
+        tc.psum_pool(name="flipped", bufs=PASSES) as flipped_pool,
+        tc.psum_pool(name="sums", bufs=TOKEN_TILES) as sums_pool,
+        tc.manual_schedule(),
+    ):
+        tokens_by_partition = hidden_states.rearrange("(p i) k -> p (i k)", p=P)
+        token_raw = []
+        for r in range(TOKEN_UNITS):
+            raw = raw_pool.tile([P, 2 * EMBED], BF16, name="token_raw%d" % r)
+            nc.sync.dma_start(out=raw[:], in_=tokens_by_partition[:, 2 * EMBED * r : 2 * EMBED * (r + 1)])
+            token_raw.append(raw)
+        weight_raw = []
+        for b in range(WEIGHT_UNITS):
+            raw = raw_pool.tile([P, 2 * EMBED], BF16, name="weight_raw%d" % b)
+            rows = Wq[UNIT_ROWS * b : UNIT_ROWS * (b + 1), :]
+            nc.sync.dma_start(out=raw[:], in_=rows.rearrange("(p a) k -> p (a k)", a=2))
+            weight_raw.append(raw)
+
+        identity = consts.tile([P, P], F32)
+        make_identity(nc, identity[:])
+        gain_bf16 = consts.tile([P, HEAD_DIM], BF16)
+        nc.scalar.dma_start(out=gain_bf16[:], in_=q_norm_w.partition_broadcast(P))
+        gain = consts.tile([P, HEAD_DIM], F32)
+        eps = consts.tile([P, 1], F32)
+        nc.vector.memset(eps[:], EPS)
+        nc.vector.tensor_copy(out=gain[:], in_=gain_bf16[:])
+        table_warmer = consts.tile([P, 1], F32)
+        nc.scalar.activation(out=table_warmer[:], in_=eps[:], func=ACT.Abs_reciprocal_sqrt)
+
+        def quantise_unit(raw, name, rows_alternate):
+            words = raw[:].bitcast(F32)
+            codes = quantised.tile([P, PASSES, UNIT_ROWS], U32, name=name + "_codes", align_bytes=64)
+            scales = quantised.tile([P, PASSES, UNIT_ROWS], U8, name=name + "_scales", align_bytes=64)
+
+            banks = []
+            for g in range(PASSES):
+                bank = flipped_pool.tile([P, 4, P], F32, name="bank")
+                for a in range(2):
+                    for u in range(2):
+                        first = ROW_WORDS * a + PASS_WORDS * g + P * u
+                        nc.tensor.transpose(bank[:, 2 * a + u, :], words[:, first : first + P], identity[:])
+                banks.append(bank)
+
+            grouped_tiles = []
+            for g in range(PASSES):
+                grouped = grouped_pool.tile([P, 4 * UNIT_ROWS], BF16, name="grouped", align_bytes=64)
+                if rows_alternate:
+                    target = grouped[:].bitcast(F32).rearrange("p (c s) -> p c s", s=4)
+                    source = banks[g][:].rearrange("p s c -> p c s")
+                else:
+                    target = grouped[:].bitcast(F32).rearrange("p (a c u) -> p a c u", a=2, u=2)
+                    source = banks[g][:].rearrange("p (a u) c -> p a c u", u=2)
+                if g == PASSES - 1:
+                    nc.vector.tensor_copy(out=target, in_=source)
+                else:
+                    nc.scalar.copy(out=target, in_=source)
+                grouped_tiles.append(grouped)
+
+            for g in range(PASSES):
+                nc.vector.quantize_mx(
+                    out=codes[:, g, :].bitcast(FP8X4), scales=scales[:, g, :], in_=grouped_tiles[g][:]
+                )
+            return codes, scales
+
+        def multiply(token_units, weight_unit):
+            weight_codes, weight_scales = weight_unit
+            groups = []
+            for i in range(TOKEN_TILES):
+                token_codes, token_scales = token_units[i // 2]
+                cols = slice(P * (i % 2), P * (i % 2) + P)
+                q = sums_pool.tile([P, UNIT_ROWS], F32, name="q")
+                for g in range(PASSES):
+                    nc.tensor.matmul_mx(
+                        out=q[:],
+                        lhsT=token_codes[:, g, cols].bitcast(FP8X4),
+                        lhsT_scale=token_scales[:, g, cols],
+                        rhs=weight_codes[:, g, :].bitcast(FP8X4),
+                        rhs_scale=weight_scales[:, g, :],
+                        start=(g == 0),
+                        stop=(g == PASSES - 1),
+                    )
+                groups.append(q)
+            return groups
+
+        out_by_partition = out.rearrange("h (p i) d -> p h (i d)", p=P)
+
+        def normalise_and_store(b, groups):
+            result = results.tile([P, UNIT_HEADS, TOKEN_TILES, HEAD_DIM], F32, name="result")
+            for first in range(0, TOKEN_TILES, 2):
+                pieces = [(i, h) for i in (first, first + 1) for h in range(UNIT_HEADS)]
+                squares = stats.tile([P, len(pieces), HEAD_DIM], F32, name="squares")
+                sum_squares = stats.tile([P, len(pieces)], F32, name="sum_squares")
+                for n, (i, h) in enumerate(pieces):
+                    nc.scalar.activation(
+                        out=squares[:, n, :],
+                        in_=groups[i][:, HEAD_DIM * h : HEAD_DIM * (h + 1)],
+                        func=ACT.Square,
+                        accum_out=sum_squares[:, n : n + 1],
+                    )
+                inv_rms = stats.tile([P, len(pieces)], F32, name="inv_rms")
+                nc.scalar.activation(
+                    out=inv_rms[:],
+                    in_=sum_squares[:],
+                    func=ACT.Abs_reciprocal_sqrt,
+                    scale=1.0 / HEAD_DIM,
+                    bias=eps[:],
+                )
+                for n, (i, h) in enumerate(pieces):
+                    nc.vector.scalar_tensor_tensor(
+                        out=result[:, h, i, :],
+                        in0=groups[i][:, HEAD_DIM * h : HEAD_DIM * (h + 1)],
+                        scalar=inv_rms[:, n : n + 1],
+                        in1=gain[:],
+                        op0=ALU.mult,
+                        op1=ALU.mult,
+                    )
+            nc.sync.dma_start(
+                out=out_by_partition[:, UNIT_HEADS * b : UNIT_HEADS * (b + 1), :],
+                in_=result[:].rearrange("p h i d -> p h (i d)"),
+            )
+
+        token_units = [quantise_unit(token_raw[r], "token%d" % r, False) for r in range(TOKEN_UNITS)]
+        weight_units = [quantise_unit(weight_raw[b], "weight%d" % b, True) for b in range(LEAD)]
+        for b in range(WEIGHT_UNITS):
+            groups = multiply(token_units, weight_units[b])
+            normalise_and_store(b, groups)
+            if b + LEAD < WEIGHT_UNITS:
+                weight_units.append(quantise_unit(weight_raw[b + LEAD], "weight%d" % (b + LEAD), True))

@@ -15,16 +15,14 @@ EPS = 1e-05
 
 K_PASS = 4 * P
 PASSES = EMBED // K_PASS
-ROW_WORDS = EMBED // 2
-PASS_WORDS = K_PASS // 2
+BANK_WORDS = 512
 
-UNIT_ROWS = 2 * P
-TOKEN_UNITS = TOKENS // UNIT_ROWS
 TOKEN_TILES = TOKENS // P
-WEIGHT_UNITS = HEADS * HEAD_DIM // UNIT_ROWS
-UNIT_HEADS = UNIT_ROWS // HEAD_DIM
-
-LEAD = 2
+UNIT_TILES = 2
+UNIT_COLS = UNIT_TILES * P
+UNIT_BANKS = UNIT_TILES * EMBED // 2 // BANK_WORDS
+TOKEN_UNITS = TOKEN_TILES // UNIT_TILES
+WEIGHT_UNITS = HEADS // UNIT_TILES
 
 FLOPS = 2 * TOKENS * EMBED * HEADS * HEAD_DIM
 
@@ -36,25 +34,37 @@ def tile_combcrossattention_pa_kernel(tc, hidden_states, Wq, q_norm_w, out):
         tc.tile_pool(name="consts", bufs=1) as consts,
         tc.tile_pool(name="raw", bufs=1) as raw_pool,
         tc.tile_pool(name="quantised", bufs=1) as quantised,
-        tc.tile_pool(name="grouped", bufs=2 * PASSES) as grouped_pool,
+        tc.tile_pool(name="grouped", bufs=4) as grouped_pool,
         tc.tile_pool(name="stats", bufs=4) as stats,
-        tc.tile_pool(name="results", bufs=3) as results,
-        tc.psum_pool(name="flipped", bufs=PASSES) as flipped_pool,
+        tc.tile_pool(name="results", bufs=6) as results,
+        tc.psum_pool(name="flipped", bufs=UNIT_BANKS) as flipped_pool,
         tc.psum_pool(name="sums", bufs=TOKEN_TILES) as sums_pool,
         tc.manual_schedule(),
     ):
-        tokens_by_partition = hidden_states.rearrange("(p i) k -> p (i k)", p=P)
-        token_raw = []
-        for r in range(TOKEN_UNITS):
-            raw = raw_pool.tile([P, 2 * EMBED], BF16, name="token_raw%d" % r)
-            nc.sync.dma_start(out=raw[:], in_=tokens_by_partition[:, 2 * EMBED * r : 2 * EMBED * (r + 1)])
-            token_raw.append(raw)
-        weight_raw = []
-        for b in range(WEIGHT_UNITS):
-            raw = raw_pool.tile([P, 2 * EMBED], BF16, name="weight_raw%d" % b)
-            rows = Wq[UNIT_ROWS * b : UNIT_ROWS * (b + 1), :]
-            nc.sync.dma_start(out=raw[:], in_=rows.rearrange("(p a) k -> p (a k)", a=2))
-            weight_raw.append(raw)
+        tokens_by_partition = hidden_states.rearrange("(p i) k -> p i k", p=P)
+
+        def load_token_unit(r):
+            tiles = []
+            for a in range(UNIT_TILES):
+                raw = raw_pool.tile([P, EMBED], BF16, name="token_raw%d" % (UNIT_TILES * r + a))
+                nc.sync.dma_start(out=raw[:], in_=tokens_by_partition[:, UNIT_TILES * r + a, :])
+                tiles.append(raw)
+            return tiles
+
+        def load_weight_unit(b):
+            tiles = []
+            for a in range(UNIT_TILES):
+                head = UNIT_TILES * b + a
+                raw = raw_pool.tile([P, EMBED], BF16, name="weight_raw%d" % head)
+                nc.sync.dma_start(out=raw[:], in_=Wq[P * head : P * (head + 1), :])
+                tiles.append(raw)
+            return tiles
+
+        token_raw = [load_token_unit(0)]
+        weight_raw = [load_weight_unit(0)]
+        token_raw.append(load_token_unit(1))
+        for b in range(1, WEIGHT_UNITS):
+            weight_raw.append(load_weight_unit(b))
 
         identity = consts.tile([P, P], F32)
         make_identity(nc, identity[:])
@@ -67,48 +77,51 @@ def tile_combcrossattention_pa_kernel(tc, hidden_states, Wq, q_norm_w, out):
         table_warmer = consts.tile([P, 1], F32)
         nc.scalar.activation(out=table_warmer[:], in_=eps[:], func=ACT.Abs_reciprocal_sqrt)
 
-        def quantise_unit(raw, name, rows_alternate):
-            words = raw[:].bitcast(F32)
-            codes = quantised.tile([P, PASSES, UNIT_ROWS], U32, name=name + "_codes", align_bytes=64)
-            scales = quantised.tile([P, PASSES, UNIT_ROWS], U8, name=name + "_scales", align_bytes=64)
+        def quantise_unit(raw_tiles, name, unit_number):
+            codes = quantised.tile([P, PASSES, UNIT_COLS], U32, name=name + "_codes", align_bytes=64)
+            scales = quantised.tile([P, PASSES, UNIT_COLS], U8, name=name + "_scales", align_bytes=64)
 
             banks = []
-            for g in range(PASSES):
-                bank = flipped_pool.tile([P, 4, P], F32, name="bank")
-                for a in range(2):
-                    for u in range(2):
-                        first = ROW_WORDS * a + PASS_WORDS * g + P * u
-                        nc.tensor.transpose(bank[:, 2 * a + u, :], words[:, first : first + P], identity[:])
-                banks.append(bank)
+            for a in range(UNIT_TILES):
+                words = raw_tiles[a][:].bitcast(F32)
+                for pair in range(PASSES // 2):
+                    bank = flipped_pool.tile([P, 4, P], F32, name="bank")
+                    for s in range(4):
+                        first = BANK_WORDS * pair + P * s
+                        nc.tensor.transpose(bank[:, s, :], words[:, first : first + P], identity[:])
+                    banks.append((a, pair, bank))
 
-            grouped_tiles = []
-            for g in range(PASSES):
-                grouped = grouped_pool.tile([P, 4 * UNIT_ROWS], BF16, name="grouped", align_bytes=64)
-                if rows_alternate:
-                    target = grouped[:].bitcast(F32).rearrange("p (c s) -> p c s", s=4)
-                    source = banks[g][:].rearrange("p s c -> p c s")
-                else:
-                    target = grouped[:].bitcast(F32).rearrange("p (a c u) -> p a c u", a=2, u=2)
-                    source = banks[g][:].rearrange("p (a u) c -> p a c u", u=2)
-                if g == PASSES - 1:
+            grouped = []
+            for pair in range(PASSES // 2):
+                grouped.append(grouped_pool.tile([P, 2 * 4 * UNIT_COLS], BF16, name="grouped", align_bytes=64))
+            for n, (a, pair, bank) in enumerate(banks):
+                target = grouped[pair][:].bitcast(F32).rearrange(
+                    "p (g a c u) -> p g a c u", g=2, a=UNIT_TILES, u=2
+                )[:, :, a]
+                source = bank[:].rearrange("p (g u) c -> p g c u", u=2)
+                if (UNIT_BANKS * unit_number + n) % 3 == 2:
                     nc.vector.tensor_copy(out=target, in_=source)
                 else:
                     nc.scalar.copy(out=target, in_=source)
-                grouped_tiles.append(grouped)
 
-            for g in range(PASSES):
+            for pair in range(PASSES // 2):
+                two_passes = slice(2 * pair, 2 * pair + 2)
                 nc.vector.quantize_mx(
-                    out=codes[:, g, :].bitcast(FP8X4), scales=scales[:, g, :], in_=grouped_tiles[g][:]
+                    out=codes[:, two_passes, :].rearrange("p g n -> p (g n)").bitcast(FP8X4),
+                    scales=scales[:, two_passes, :].rearrange("p g n -> p (g n)"),
+                    in_=grouped[pair][:],
                 )
             return codes, scales
 
-        def multiply(token_units, weight_unit):
+        out_by_partition = out.rearrange("h (p i) d -> p h i d", p=P)
+
+        def product(b, r, weight_unit, token_unit):
             weight_codes, weight_scales = weight_unit
+            token_codes, token_scales = token_unit
             groups = []
-            for i in range(TOKEN_TILES):
-                token_codes, token_scales = token_units[i // 2]
-                cols = slice(P * (i % 2), P * (i % 2) + P)
-                q = sums_pool.tile([P, UNIT_ROWS], F32, name="q")
+            for a in range(UNIT_TILES):
+                cols = slice(P * a, P * (a + 1))
+                q = sums_pool.tile([P, UNIT_COLS], F32, name="q")
                 for g in range(PASSES):
                     nc.tensor.matmul_mx(
                         out=q[:],
@@ -120,49 +133,50 @@ def tile_combcrossattention_pa_kernel(tc, hidden_states, Wq, q_norm_w, out):
                         stop=(g == PASSES - 1),
                     )
                 groups.append(q)
-            return groups
 
-        out_by_partition = out.rearrange("h (p i) d -> p h (i d)", p=P)
-
-        def normalise_and_store(b, groups):
-            result = results.tile([P, UNIT_HEADS, TOKEN_TILES, HEAD_DIM], F32, name="result")
-            for first in range(0, TOKEN_TILES, 2):
-                pieces = [(i, h) for i in (first, first + 1) for h in range(UNIT_HEADS)]
-                squares = stats.tile([P, len(pieces), HEAD_DIM], F32, name="squares")
-                sum_squares = stats.tile([P, len(pieces)], F32, name="sum_squares")
-                for n, (i, h) in enumerate(pieces):
-                    nc.scalar.activation(
-                        out=squares[:, n, :],
-                        in_=groups[i][:, HEAD_DIM * h : HEAD_DIM * (h + 1)],
-                        func=ACT.Square,
-                        accum_out=sum_squares[:, n : n + 1],
-                    )
-                inv_rms = stats.tile([P, len(pieces)], F32, name="inv_rms")
+            pieces = [(a, h) for a in range(UNIT_TILES) for h in range(UNIT_TILES)]
+            squares = stats.tile([P, len(pieces), HEAD_DIM], F32, name="squares")
+            sum_squares = stats.tile([P, len(pieces)], F32, name="sum_squares")
+            for n, (a, h) in enumerate(pieces):
                 nc.scalar.activation(
-                    out=inv_rms[:],
-                    in_=sum_squares[:],
-                    func=ACT.Abs_reciprocal_sqrt,
-                    scale=1.0 / HEAD_DIM,
-                    bias=eps[:],
+                    out=squares[:, n, :],
+                    in_=groups[a][:, HEAD_DIM * h : HEAD_DIM * (h + 1)],
+                    func=ACT.Square,
+                    accum_out=sum_squares[:, n : n + 1],
                 )
-                for n, (i, h) in enumerate(pieces):
-                    nc.vector.scalar_tensor_tensor(
-                        out=result[:, h, i, :],
-                        in0=groups[i][:, HEAD_DIM * h : HEAD_DIM * (h + 1)],
-                        scalar=inv_rms[:, n : n + 1],
-                        in1=gain[:],
-                        op0=ALU.mult,
-                        op1=ALU.mult,
-                    )
+            inv_rms = stats.tile([P, len(pieces)], F32, name="inv_rms")
+            nc.scalar.activation(
+                out=inv_rms[:],
+                in_=sum_squares[:],
+                func=ACT.Abs_reciprocal_sqrt,
+                scale=1.0 / HEAD_DIM,
+                bias=eps[:],
+            )
+            result = results.tile([P, UNIT_TILES, UNIT_TILES, HEAD_DIM], F32, name="result")
+            for n, (a, h) in enumerate(pieces):
+                nc.vector.scalar_tensor_tensor(
+                    out=result[:, h, a, :],
+                    in0=groups[a][:, HEAD_DIM * h : HEAD_DIM * (h + 1)],
+                    scalar=inv_rms[:, n : n + 1],
+                    in1=gain[:],
+                    op0=ALU.mult,
+                    op1=ALU.mult,
+                )
             nc.sync.dma_start(
-                out=out_by_partition[:, UNIT_HEADS * b : UNIT_HEADS * (b + 1), :],
-                in_=result[:].rearrange("p h i d -> p h (i d)"),
+                out=out_by_partition[
+                    :, UNIT_TILES * b : UNIT_TILES * (b + 1), UNIT_TILES * r : UNIT_TILES * (r + 1), :
+                ],
+                in_=result[:],
             )
 
-        token_units = [quantise_unit(token_raw[r], "token%d" % r, False) for r in range(TOKEN_UNITS)]
-        weight_units = [quantise_unit(weight_raw[b], "weight%d" % b, True) for b in range(LEAD)]
-        for b in range(WEIGHT_UNITS):
-            groups = multiply(token_units, weight_units[b])
-            normalise_and_store(b, groups)
-            if b + LEAD < WEIGHT_UNITS:
-                weight_units.append(quantise_unit(weight_raw[b + LEAD], "weight%d" % (b + LEAD), True))
+        token_units = [quantise_unit(token_raw[0], "token0", 0)]
+        weight_units = [quantise_unit(weight_raw[0], "weight0", 1)]
+        token_units.append(quantise_unit(token_raw[1], "token1", 2))
+        product(0, 0, weight_units[0], token_units[0])
+        weight_units.append(quantise_unit(weight_raw[1], "weight1", 3))
+        product(0, 1, weight_units[0], token_units[1])
+        for b in range(1, WEIGHT_UNITS):
+            if b + 1 < WEIGHT_UNITS:
+                weight_units.append(quantise_unit(weight_raw[b + 1], "weight%d" % (b + 1), b + 3))
+            for r in range(TOKEN_UNITS):
+                product(b, r, weight_units[b], token_units[r])

@@ -68,12 +68,20 @@ def tile_combcrossattention_pa_kernel(tc, hidden_states, Wq, q_norm_w, out):
 
         identity = consts.tile([P, P], F32)
         make_identity(nc, identity[:])
-        gain_bf16 = consts.tile([P, HEAD_DIM], BF16)
-        nc.scalar.dma_start(out=gain_bf16[:], in_=q_norm_w.partition_broadcast(P))
+        gain_row = consts.tile([P, HEAD_DIM], BF16)
+        nc.vector.memset(gain_row[:], 0.0)
+        nc.scalar.dma_start(out=gain_row[0:1, :], in_=q_norm_w.unsqueeze(0))
+        ones = consts.tile([P, P], BF16)
+        nc.vector.memset(ones[:], 1.0)
         gain = consts.tile([P, HEAD_DIM], F32)
         eps = consts.tile([P, 1], F32)
         nc.vector.memset(eps[:], EPS)
-        nc.vector.tensor_copy(out=gain[:], in_=gain_bf16[:])
+
+        def spread_gain():
+            bank = flipped_pool.tile([P, 4, P], F32, name="bank")
+            nc.tensor.matmul(out=bank[:, 0, :], lhsT=ones[:], rhs=gain_row[:], start=True, stop=True)
+            nc.vector.tensor_copy(out=gain[:], in_=bank[:, 0, :])
+
         table_warmer = consts.tile([P, 1], F32)
         nc.scalar.activation(out=table_warmer[:], in_=eps[:], func=ACT.Abs_reciprocal_sqrt)
 
@@ -170,6 +178,7 @@ def tile_combcrossattention_pa_kernel(tc, hidden_states, Wq, q_norm_w, out):
             )
 
         token_units = [quantise_unit(token_raw[0], "token0", 0)]
+        spread_gain()
         weight_units = [quantise_unit(weight_raw[0], "weight0", 1)]
         token_units.append(quantise_unit(token_raw[1], "token1", 2))
         product(0, 0, weight_units[0], token_units[0])

@@ -24,6 +24,12 @@ UNIT_BANKS = UNIT_TILES * EMBED // 2 // BANK_WORDS
 TOKEN_UNITS = TOKEN_TILES // UNIT_TILES
 WEIGHT_UNITS = HEADS // UNIT_TILES
 
+RESULT_BUFS = TOKEN_UNITS * WEIGHT_UNITS
+
+IDLE_MATMULS_AT_START = 6
+IDLE_MATMULS_A_UNIT = 3
+IDLE_COLS = 512
+
 FLOPS = 2 * TOKENS * EMBED * HEADS * HEAD_DIM
 
 
@@ -36,7 +42,7 @@ def tile_combcrossattention_pa_kernel(tc, hidden_states, Wq, q_norm_w, out):
         tc.tile_pool(name="quantised", bufs=1) as quantised,
         tc.tile_pool(name="grouped", bufs=4) as grouped_pool,
         tc.tile_pool(name="stats", bufs=4) as stats,
-        tc.tile_pool(name="results", bufs=6) as results,
+        tc.tile_pool(name="results", bufs=RESULT_BUFS) as results,
         tc.psum_pool(name="flipped", bufs=UNIT_BANKS) as flipped_pool,
         tc.psum_pool(name="sums", bufs=TOKEN_TILES) as sums_pool,
         tc.manual_schedule(),
@@ -76,6 +82,14 @@ def tile_combcrossattention_pa_kernel(tc, hidden_states, Wq, q_norm_w, out):
         gain = consts.tile([P, HEAD_DIM], F32)
         eps = consts.tile([P, 1], F32)
         nc.vector.memset(eps[:], EPS)
+
+        idle_rhs = consts.tile([P, IDLE_COLS], BF16)
+        nc.vector.memset(idle_rhs[:], 0.0)
+
+        def keep_clock_up(count):
+            unread = sums_pool.tile([P, IDLE_COLS], F32, name="unread", tag="q")
+            for n in range(count):
+                nc.tensor.matmul(out=unread[:], lhsT=ones[:], rhs=idle_rhs[:], start=True, stop=True)
 
         def spread_gain():
             bank = flipped_pool.tile([P, 4, P], F32, name="bank")
@@ -177,9 +191,12 @@ def tile_combcrossattention_pa_kernel(tc, hidden_states, Wq, q_norm_w, out):
                 in_=result[:],
             )
 
+        keep_clock_up(IDLE_MATMULS_AT_START)
         token_units = [quantise_unit(token_raw[0], "token0", 0)]
-        spread_gain()
+        keep_clock_up(IDLE_MATMULS_A_UNIT)
         weight_units = [quantise_unit(weight_raw[0], "weight0", 1)]
+        spread_gain()
+        keep_clock_up(IDLE_MATMULS_A_UNIT)
         token_units.append(quantise_unit(token_raw[1], "token1", 2))
         product(0, 0, weight_units[0], token_units[0])
         weight_units.append(quantise_unit(weight_raw[1], "weight1", 3))

@@ -26,10 +26,6 @@ WEIGHT_UNITS = HEADS // UNIT_TILES
 
 RESULT_BUFS = TOKEN_UNITS * WEIGHT_UNITS
 
-IDLE_MATMULS_AT_START = 6
-IDLE_MATMULS_A_UNIT = 3
-IDLE_COLS = 512
-
 FLOPS = 2 * TOKENS * EMBED * HEADS * HEAD_DIM
 
 
@@ -82,14 +78,6 @@ def tile_combcrossattention_pa_kernel(tc, hidden_states, Wq, q_norm_w, out):
         gain = consts.tile([P, HEAD_DIM], F32)
         eps = consts.tile([P, 1], F32)
         nc.vector.memset(eps[:], EPS)
-
-        idle_rhs = consts.tile([P, IDLE_COLS], BF16)
-        nc.vector.memset(idle_rhs[:], 0.0)
-
-        def keep_clock_up(count):
-            unread = sums_pool.tile([P, IDLE_COLS], F32, name="unread", tag="q")
-            for n in range(count):
-                nc.tensor.matmul(out=unread[:], lhsT=ones[:], rhs=idle_rhs[:], start=True, stop=True)
 
         def spread_gain():
             bank = flipped_pool.tile([P, 4, P], F32, name="bank")
@@ -191,12 +179,9 @@ def tile_combcrossattention_pa_kernel(tc, hidden_states, Wq, q_norm_w, out):
                 in_=result[:],
             )
 
-        keep_clock_up(IDLE_MATMULS_AT_START)
         token_units = [quantise_unit(token_raw[0], "token0", 0)]
-        keep_clock_up(IDLE_MATMULS_A_UNIT)
         weight_units = [quantise_unit(weight_raw[0], "weight0", 1)]
         spread_gain()
-        keep_clock_up(IDLE_MATMULS_A_UNIT)
         token_units.append(quantise_unit(token_raw[1], "token1", 2))
         product(0, 0, weight_units[0], token_units[0])
         weight_units.append(quantise_unit(weight_raw[1], "weight1", 3))

import concourse.mybir as mybir
from concourse.masks import make_identity

F32 = mybir.dt.float32
BF16 = mybir.dt.bfloat16
U32 = mybir.dt.uint32
U8 = mybir.dt.uint8
FP8X4 = mybir.dt.float8_e4m3fn_x4
ACT = mybir.ActivationFunctionType
ALU = mybir.AluOpType

P = 128
TOKENS, EMBED, HEADS, HEAD_DIM = 512, 2048, 16, 128
EPS = 1e-05

K_PASS = 4 * P
PASSES = EMBED // K_PASS
BANK_WORDS = 512

TOKEN_TILES = TOKENS // P
UNIT_TILES = 2
UNIT_COLS = UNIT_TILES * P
UNIT_BANKS = UNIT_TILES * EMBED // 2 // BANK_WORDS
TOKEN_UNITS = TOKEN_TILES // UNIT_TILES
WEIGHT_UNITS = HEADS // UNIT_TILES

RESULT_BUFS = TOKEN_UNITS * WEIGHT_UNITS

FLOPS = 2 * TOKENS * EMBED * HEADS * HEAD_DIM


def tile_combcrossattention_pa_kernel(tc, hidden_states, Wq, q_norm_w, out):
    nc = tc.nc

    with (
        tc.tile_pool(name="consts", bufs=1) as consts,
        tc.tile_pool(name="raw", bufs=1) as raw_pool,
        tc.tile_pool(name="quantised", bufs=1) as quantised,
        tc.tile_pool(name="grouped", bufs=4) as grouped_pool,
        tc.tile_pool(name="stats", bufs=4) as stats,
        tc.tile_pool(name="results", bufs=RESULT_BUFS) as results,
        tc.psum_pool(name="flipped", bufs=UNIT_BANKS) as flipped_pool,
        tc.psum_pool(name="sums", bufs=TOKEN_TILES) as sums_pool,
        tc.manual_schedule(),
    ):
        tokens_by_partition = hidden_states.rearrange("(p i) k -> p i k", p=P)

        def load_token_unit(r):
            tiles = []
            for a in range(UNIT_TILES):
                raw = raw_pool.tile([P, EMBED], BF16, name="token_raw%d" % (UNIT_TILES * r + a))
                nc.sync.dma_start(out=raw[:], in_=tokens_by_partition[:, UNIT_TILES * r + a, :])
                tiles.append(raw)
            return tiles

        def load_weight_unit(b):
            tiles = []
            for a in range(UNIT_TILES):
                head = UNIT_TILES * b + a
                raw = raw_pool.tile([P, EMBED], BF16, name="weight_raw%d" % head)
                nc.sync.dma_start(out=raw[:], in_=Wq[P * head : P * (head + 1), :])
                tiles.append(raw)
            return tiles

        token_raw = [load_token_unit(0)]
        weight_raw = [load_weight_unit(0)]
        token_raw.append(load_token_unit(1))
        for b in range(1, WEIGHT_UNITS):
            weight_raw.append(load_weight_unit(b))

        identity = consts.tile([P, P], F32)
        make_identity(nc, identity[:])
        gain_row = consts.tile([P, HEAD_DIM], BF16)
        nc.vector.memset(gain_row[:], 0.0)
        nc.scalar.dma_start(out=gain_row[0:1, :], in_=q_norm_w.unsqueeze(0))
        ones = consts.tile([P, P], BF16)
        nc.vector.memset(ones[:], 1.0)
        gain = consts.tile([P, HEAD_DIM], F32)
        eps = consts.tile([P, 1], F32)
        nc.vector.memset(eps[:], EPS)

        def spread_gain():
            bank = flipped_pool.tile([P, 4, P], F32, name="bank")
            nc.tensor.matmul(out=bank[:, 0, :], lhsT=ones[:], rhs=gain_row[:], start=True, stop=True)
            nc.vector.tensor_copy(out=gain[:], in_=bank[:, 0, :])

        table_warmer = consts.tile([P, 1], F32)
        nc.scalar.activation(out=table_warmer[:], in_=eps[:], func=ACT.Abs_reciprocal_sqrt)

        def quantise_unit(raw_tiles, name, unit_number):
            codes = quantised.tile([P, PASSES, UNIT_COLS], U32, name=name + "_codes", align_bytes=64)
            scales = quantised.tile([P, PASSES, UNIT_COLS], U8, name=name + "_scales", align_bytes=64)

            banks = []
            for a in range(UNIT_TILES):
                words = raw_tiles[a][:].bitcast(F32)
                for pair in range(PASSES // 2):
                    bank = flipped_pool.tile([P, 4, P], F32, name="bank")
                    for s in range(4):
                        first = BANK_WORDS * pair + P * s
                        nc.tensor.transpose(bank[:, s, :], words[:, first : first + P], identity[:])
                    banks.append((a, pair, bank))

            grouped = []
            for pair in range(PASSES // 2):
                grouped.append(grouped_pool.tile([P, 2 * 4 * UNIT_COLS], BF16, name="grouped", align_bytes=64))
            for n, (a, pair, bank) in enumerate(banks):
                target = grouped[pair][:].bitcast(F32).rearrange(
                    "p (g a c u) -> p g a c u", g=2, a=UNIT_TILES, u=2
                )[:, :, a]
                source = bank[:].rearrange("p (g u) c -> p g c u", u=2)
                if (UNIT_BANKS * unit_number + n) % 3 == 2:
                    nc.vector.tensor_copy(out=target, in_=source)
                else:
                    nc.scalar.copy(out=target, in_=source)

            for pair in range(PASSES // 2):
                two_passes = slice(2 * pair, 2 * pair + 2)
                nc.vector.quantize_mx(
                    out=codes[:, two_passes, :].rearrange("p g n -> p (g n)").bitcast(FP8X4),
                    scales=scales[:, two_passes, :].rearrange("p g n -> p (g n)"),
                    in_=grouped[pair][:],
                )
            return codes, scales

        out_by_partition = out.rearrange("h (p i) d -> p h i d", p=P)

        def product(b, r, weight_unit, token_unit):
            weight_codes, weight_scales = weight_unit
            token_codes, token_scales = token_unit
            groups = []
            for a in range(UNIT_TILES):
                cols = slice(P * a, P * (a + 1))
                q = sums_pool.tile([P, UNIT_COLS], F32, name="q")
                for g in range(PASSES):
                    nc.tensor.matmul_mx(
                        out=q[:],
                        lhsT=token_codes[:, g, cols].bitcast(FP8X4),
                        lhsT_scale=token_scales[:, g, cols],
                        rhs=weight_codes[:, g, :].bitcast(FP8X4),
                        rhs_scale=weight_scales[:, g, :],
                        start=(g == 0),
                        stop=(g == PASSES - 1),
                    )
                groups.append(q)

            pieces = [(a, h) for a in range(UNIT_TILES) for h in range(UNIT_TILES)]
            squares = stats.tile([P, len(pieces), HEAD_DIM], F32, name="squares")
            sum_squares = stats.tile([P, len(pieces)], F32, name="sum_squares")
            for n, (a, h) in enumerate(pieces):
                nc.scalar.activation(
                    out=squares[:, n, :],
                    in_=groups[a][:, HEAD_DIM * h : HEAD_DIM * (h + 1)],
                    func=ACT.Square,
                    accum_out=sum_squares[:, n : n + 1],
                )
            inv_rms = stats.tile([P, len(pieces)], F32, name="inv_rms")
            nc.scalar.activation(
                out=inv_rms[:],
                in_=sum_squares[:],
                func=ACT.Abs_reciprocal_sqrt,
                scale=1.0 / HEAD_DIM,
                bias=eps[:],
            )
            result = results.tile([P, UNIT_TILES, UNIT_TILES, HEAD_DIM], F32, name="result")
            for n, (a, h) in enumerate(pieces):
                nc.vector.scalar_tensor_tensor(
                    out=result[:, h, a, :],
                    in0=groups[a][:, HEAD_DIM * h : HEAD_DIM * (h + 1)],
                    scalar=inv_rms[:, n : n + 1],
                    in1=gain[:],
                    op0=ALU.mult,
                    op1=ALU.mult,
                )
            nc.sync.dma_start(
                out=out_by_partition[
                    :, UNIT_TILES * b : UNIT_TILES * (b + 1), UNIT_TILES * r : UNIT_TILES * (r + 1), :
                ],
                in_=result[:],
            )

        token_units = [quantise_unit(token_raw[0], "token0", 0)]
        weight_units = [quantise_unit(weight_raw[0], "weight0", 1)]
        spread_gain()
        token_units.append(quantise_unit(token_raw[1], "token1", 2))
        product(0, 0, weight_units[0], token_units[0])
        weight_units.append(quantise_unit(weight_raw[1], "weight1", 3))
        product(0, 1, weight_units[0], token_units[1])
        for b in range(1, WEIGHT_UNITS):
            if b + 1 < WEIGHT_UNITS:
                weight_units.append(quantise_unit(weight_raw[b + 1], "weight%d" % (b + 1), b + 3))
            for r in range(TOKEN_UNITS):
                product(b, r, weight_units[b], token_units[r])
